import numpy as np
import ml_dtypes


def mxq(x, axis, fmt="e4m3"):
    dtype, down = {"e4m3": (ml_dtypes.float8_e4m3fn, 7), "e5m2": (ml_dtypes.float8_e5m2, 14)}[fmt]
    v = np.moveaxis(np.asarray(x, np.float32).astype(ml_dtypes.bfloat16).astype(np.float64), axis, -1)
    blocks = v.reshape(v.shape[:-1] + (-1, 32))
    amax = np.abs(blocks).max(-1, keepdims=True)
    byte = np.maximum(np.where(amax > 0, np.frexp(amax)[1] - 1 + 127, 0) - down, 1)
    scale = np.exp2(byte - 127.0)
    codes = (blocks / scale).astype(np.float32).astype(dtype).astype(np.float64)
    return np.moveaxis((codes * scale).reshape(v.shape), -1, axis)


WIDE = False


def mx_kscale(k):
    if not WIDE:
        return np.ones(k)
    levels = np.array([10, -10, 5, -5, 0])
    if k % 512:
        return np.exp2(np.random.permutation(np.resize(levels, k // 32))).repeat(32)
    a = np.empty((k // 512, 16))
    for p in range(k // 512):
        a[p, :8] = np.random.permutation(np.resize(levels, 8))
        for g in range(8):
            far = levels[np.abs(levels - a[p, g]) >= 10]
            a[p, g + 8] = far[np.random.randint(len(far))]
    return np.exp2(a.ravel()).repeat(32)


BF16 = ml_dtypes.bfloat16


def bf(x):
    return np.asarray(x, np.float32).astype(BF16)


def f64(x):
    return np.asarray(x).astype(np.float64)


B, DIN, H0, H1, L, C, K = 128, 1024, 2048, 1024, 512, 32, 64
BETA = 10.0


def logsumexp(a):
    m = a.max(-1, keepdims=True)
    return (m + np.log(np.exp(a - m).sum(-1, keepdims=True)))[..., 0]


def setup_inputs():
    s, t = mx_kscale(H1), mx_kscale(L)
    return {"h_enc": bf(np.maximum(np.random.standard_normal((B, H1)), 0.0) * s),
            "enc_w2": bf(np.random.standard_normal((H1, L)) * np.sqrt(2.0 / H1) / s[:, None] * t),
            "enc_b2": bf(np.random.standard_normal(L) * 0.1 * t),
            "clus_w": bf(np.random.standard_normal((C, K, L)) * 0.3 / np.sqrt(L) / t),
            "clus_b": bf(np.random.standard_normal((C, K)) * 0.1)}


def reference(h_enc, enc_w2, enc_b2, clus_w, clus_b):
    z = (mxq(f64(h_enc), 1, "e4m3") @ mxq(f64(enc_w2), 0, "e4m3")) + f64(enc_b2)
    wq = mxq(f64(clus_w), 2, "e4m3")
    scores = (mxq(z, 1, "e4m3") @ wq.reshape(C * K, L).T).reshape(B, C, K) + f64(clus_b)
    conf = -logsumexp(-BETA * scores)
    return z, conf

@@ -1,0 +1,275 @@
+from contextlib import ExitStack
+
+import concourse.mybir as mybir
+from concourse.masks import make_identity
+
+F32 = mybir.dt.float32
+BF16 = mybir.dt.bfloat16
+U32 = mybir.dt.uint32
+U8 = mybir.dt.uint8
+FP8X4 = mybir.dt.float8_e4m3fn_x4
+ALU = mybir.AluOpType
+ACT = mybir.ActivationFunctionType
+AXIS = mybir.AxisListType
+
+P = 128
+PACK = 4
+K_PASS = P * PACK
+HIDDEN = 1024
+LATENT = 512
+MODULES = 32
+HEADS = 64
+BETA = 10.0
+
+HIDDEN_PASSES = HIDDEN // K_PASS
+LATENT_TILES = LATENT // P
+CHUNK_ROWS = 512
+CHUNKS = MODULES * HEADS // CHUNK_ROWS
+ROWS_PER_PARTITION = CHUNK_ROWS // P
+CHUNK_MODULES = CHUNK_ROWS // HEADS
+GROUP_MODULES = CHUNK_MODULES // 2
+
+FLOPS = 2 * P * HIDDEN * LATENT + 2 * P * LATENT * MODULES * HEADS
+
+
+def tile_ace_pa_s_kernel(tc, h_enc, enc_w2, enc_b2, clus_w, clus_b, z_out, conf_out):
+    nc = tc.nc
+    with ExitStack() as stack:
+        keep = stack.enter_context(tc.tile_pool(name="keep", bufs=1))
+        psum_t = stack.enter_context(tc.psum_pool(name="psum_t", bufs=4))
+        psum_mx = stack.enter_context(tc.psum_pool(name="psum_mx", bufs=4))
+
+        cb_bf16 = keep.tile([P, CHUNKS, ROWS_PER_PARTITION], BF16)
+        nc.sync.dma_start(
+            out=cb_bf16[:],
+            in_=clus_b.rearrange("c k -> (c k)").rearrange(
+                "(j p r) -> p j r", j=CHUNKS, r=ROWS_PER_PARTITION
+            ),
+        )
+        w2_rows = []
+        for g in range(HIDDEN_PASSES):
+            rows = keep.tile([P, PACK, LATENT], BF16, name="w2_rows%d" % g)
+            nc.sync.dma_start(
+                out=rows[:],
+                in_=enc_w2[g * K_PASS : (g + 1) * K_PASS, :].rearrange("(q t) d -> q t d", t=PACK),
+            )
+            w2_rows.append(rows)
+        h_rows = keep.tile([P, HIDDEN], BF16)
+        nc.sync.dma_start(out=h_rows[:], in_=h_enc)
+        b2_bf16 = keep.tile([P, PACK], BF16)
+        nc.sync.dma_start(
+            out=b2_bf16[:],
+            in_=enc_b2.rearrange("(q t) -> q t", t=PACK),
+        )
+        clus_w_rows = clus_w.rearrange("c k d -> (c k) d")
+        cw_rows = []
+        for j in range(CHUNKS):
+            rows = keep.tile([P, ROWS_PER_PARTITION * LATENT], BF16, name="cw_rows%d" % j)
+            nc.sync.dma_start(
+                out=rows[:],
+                in_=clus_w_rows[j * CHUNK_ROWS : (j + 1) * CHUNK_ROWS, :].rearrange(
+                    "(p r) d -> p (r d)", r=ROWS_PER_PARTITION
+                ),
+            )
+            cw_rows.append(rows)
+
+        identity = keep.tile([P, P], F32)
+        make_identity(nc, identity[:])
+        one_column = keep.tile([P, 1], F32)
+        nc.vector.memset(one_column[:], 0.0)
+        table_warmer = keep.tile([P, 1], F32)
+        nc.scalar.activation(out=table_warmer[:], in_=one_column[:], func=ACT.Exp)
+
+        cb_scaled = keep.tile([P, CHUNKS, ROWS_PER_PARTITION], F32)
+        nc.vector.tensor_scalar_mul(out=cb_scaled[:], in0=cb_bf16[:], scalar1=-BETA)
+        bias_rows = []
+        for j in range(CHUNKS):
+            spread = psum_t.tile([P, ROWS_PER_PARTITION, P], F32, tag="t")
+            for r in range(ROWS_PER_PARTITION):
+                nc.tensor.transpose(
+                    spread[:, r, :], cb_scaled[:, j, r : r + 1].to_broadcast([P, P]), identity[:]
+                )
+            rows = keep.tile([P, CHUNK_ROWS], F32, name="bias_rows%d" % j)
+            nc.scalar.copy(out=rows[:], in_=spread[:].rearrange("b r p -> b (r p)"))
+            bias_rows.append(rows)
+
+        w2_grouped = []
+        for g in range(HIDDEN_PASSES):
+            grouped = keep.tile([P, LATENT * PACK], BF16, align_bytes=64, name="w2_grouped%d" % g)
+            nc.vector.tensor_copy(
+                out=grouped[:].rearrange("p (t q j) -> p t q j", t=PACK, j=PACK),
+                in_=w2_rows[g][:].rearrange("p j (q t) -> p t q j", t=PACK),
+            )
+            w2_grouped.append(grouped)
+        w2_codes = []
+        w2_scales = []
+        for g in range(HIDDEN_PASSES):
+            codes = keep.tile([P, LATENT], U32, align_bytes=64, name="w2_codes%d" % g)
+            scales = keep.tile([P, LATENT], U8, align_bytes=64, name="w2_scales%d" % g)
+            nc.vector.quantize_mx(out=codes[:].bitcast(FP8X4), scales=scales[:], in_=w2_grouped[g][:])
+            w2_codes.append(codes)
+            w2_scales.append(scales)
+
+        h_words = h_rows[:].bitcast(F32)
+        h_wordsT = psum_t.tile([P, HIDDEN_PASSES, 2, P], F32, tag="t")
+        for g in range(HIDDEN_PASSES):
+            for u in range(2):
+                every_2nd = slice(2 * g * P + u, 2 * (g + 1) * P, 2)
+                nc.tensor.transpose(h_wordsT[:, g, u, :], h_words[:, every_2nd], identity[:])
+        h_grouped = keep.tile([P, HIDDEN_PASSES * P * PACK], BF16, align_bytes=64)
+        nc.scalar.copy(
+            out=h_grouped[:].bitcast(F32).rearrange("q (g b u) -> q g b u", g=HIDDEN_PASSES, u=2),
+            in_=h_wordsT[:].rearrange("q g u b -> q g b u"),
+        )
+        b2 = keep.tile([P, PACK], F32)
+        nc.vector.tensor_copy(out=b2[:], in_=b2_bf16[:])
+        h_codes = keep.tile([P, HIDDEN_PASSES * P], U32, align_bytes=64)
+        h_scales = keep.tile([P, HIDDEN_PASSES * P], U8, align_bytes=64)
+        nc.vector.quantize_mx(out=h_codes[:].bitcast(FP8X4), scales=h_scales[:], in_=h_grouped[:])
+
+        cw_grouped = [
+            keep.tile([P, CHUNK_ROWS * PACK], BF16, align_bytes=64, name="cw_grouped%d" % j)
+            for j in range(CHUNKS)
+        ]
+        cw_codes = [
+            keep.tile([P, CHUNK_ROWS], U32, align_bytes=64, name="cw_codes%d" % j) for j in range(CHUNKS)
+        ]
+        cw_scales = [
+            keep.tile([P, CHUNK_ROWS], U8, align_bytes=64, name="cw_scales%d" % j) for j in range(CHUNKS)
+        ]
+        scaled = [keep.tile([P, CHUNK_ROWS], F32, name="scaled%d" % j) for j in range(CHUNKS)]
+        neg_max = keep.tile([P, MODULES], F32)
+        exp_sum = keep.tile([P, MODULES], F32)
+
+        def by_module(columns):
+            return columns.rearrange("b (r m i) -> b m r i", r=ROWS_PER_PARTITION, m=CHUNK_MODULES)
+
+        def by_row(columns):
+            return columns.rearrange("b (r m i) -> b r m i", r=ROWS_PER_PARTITION, m=CHUNK_MODULES)
+
+        def transpose_chunk(j):
+            words = cw_rows[j][:].bitcast(F32)
+            grouped_words = cw_grouped[j][:].bitcast(F32).rearrange(
+                "q (r p u) -> q r p u", r=ROWS_PER_PARTITION, u=2
+            )
+            for half in range(2):
+                wordsT = psum_t.tile([P, 2, 2, P], F32, tag="t")
+                for r in range(2):
+                    for u in range(2):
+                        row = 2 * half + r
+                        every_2nd = slice(2 * row * P + u, 2 * (row + 1) * P, 2)
+                        nc.tensor.transpose(wordsT[:, r, u, :], words[:, every_2nd], identity[:])
+                nc.scalar.copy(
+                    out=grouped_words[:, 2 * half : 2 * half + 2, :, :],
+                    in_=wordsT[:].rearrange("q r u p -> q r p u"),
+                )
+
+        def quantise_chunk(j):
+            nc.vector.quantize_mx(
+                out=cw_codes[j][:].bitcast(FP8X4), scales=cw_scales[j][:], in_=cw_grouped[j][:]
+            )
+
+        def score_chunk(j):
+            sums = psum_mx.tile([P, CHUNK_ROWS], F32, tag="mx")
+            nc.tensor.matmul_mx(
+                out=sums[:],
+                lhsT=z_codes[:].bitcast(FP8X4),
+                lhsT_scale=z_scales[:],
+                rhs=cw_codes[j][:].bitcast(FP8X4),
+                rhs_scale=cw_scales[j][:],
+                start=True,
+                stop=True,
+            )
+            for first in range(0, CHUNK_MODULES, GROUP_MODULES):
+                group = slice(first, first + GROUP_MODULES)
+                nc.vector.scalar_tensor_tensor(
+                    out=by_row(scaled[j][:])[:, :, group, :].rearrange("b r m i -> b r (m i)"),
+                    in0=by_row(sums[:])[:, :, group, :].rearrange("b r m i -> b r (m i)"),
+                    scalar=-BETA,
+                    in1=by_row(bias_rows[j][:])[:, :, group, :].rearrange("b r m i -> b r (m i)"),
+                    op0=ALU.mult,
+                    op1=ALU.add,
+                )
+            for first in range(0, CHUNK_MODULES, GROUP_MODULES):
+                c = j * CHUNK_MODULES + first
+                nc.vector.tensor_reduce(
+                    out=neg_max[:, c : c + GROUP_MODULES],
+                    in_=by_module(scaled[j][:])[:, first : first + GROUP_MODULES, :, :],
+                    axis=AXIS.XY,
+                    op=ALU.max,
+                    negate=True,
+                )
+
+        def sum_exps_chunk(j):
+            exps = keep.tile([P, CHUNK_ROWS], F32, name="exps%d" % j)
+            for m in range(CHUNK_MODULES):
+                c = j * CHUNK_MODULES + m
+                nc.scalar.activation(
+                    out=by_module(exps[:])[:, m, :, :],
+                    in_=by_module(scaled[j][:])[:, m, :, :],
+                    func=ACT.Exp,
+                    bias=neg_max[:, c : c + 1],
+                    accum_out=exp_sum[:, c : c + 1],
+                )
+
+        transpose_chunk(0)
+
+        zT_sums = psum_mx.tile([P, LATENT_TILES, P], F32, tag="mx")
+        for t in range(LATENT_TILES):
+            for g in range(HIDDEN_PASSES):
+                nc.tensor.matmul_mx(
+                    out=zT_sums[:, t, :],
+                    lhsT=w2_codes[g][:, t * P : (t + 1) * P].bitcast(FP8X4),
+                    lhsT_scale=w2_scales[g][:, t * P : (t + 1) * P],
+                    rhs=h_codes[:, g * P : (g + 1) * P].bitcast(FP8X4),
+                    rhs_scale=h_scales[:, g * P : (g + 1) * P],
+                    start=(g == 0),
+                    stop=(g == HIDDEN_PASSES - 1),
+                )
+
+        transpose_chunk(1)
+
+        z_grouped = keep.tile([P, P * PACK], BF16, align_bytes=64)
+        nc.vector.tensor_tensor(
+            out=z_grouped[:].rearrange("q (b t) -> q b t", t=PACK),
+            in0=zT_sums[:].rearrange("q t b -> q b t"),
+            in1=b2[:].unsqueeze(1).to_broadcast([P, P, PACK]),
+            op=ALU.add,
+        )
+        quantise_chunk(0)
+        z_codes = keep.tile([P, P], U32, align_bytes=64)
+        z_scales = keep.tile([P, P], U8, align_bytes=64)
+        nc.vector.quantize_mx(out=z_codes[:].bitcast(FP8X4), scales=z_scales[:], in_=z_grouped[:])
+        quantise_chunk(1)
+
+        zT = keep.tile([P, LATENT_TILES, P], F32)
+        for t in range(LATENT_TILES):
+            nc.scalar.activation(
+                out=zT[:, t, :], in_=zT_sums[:, t, :], func=ACT.Identity, bias=b2[:, t : t + 1]
+            )
+
+        for j in range(CHUNKS):
+            if j + 2 < CHUNKS:
+                transpose_chunk(j + 2)
+            score_chunk(j)
+            if j + 2 < CHUNKS:
+                quantise_chunk(j + 2)
+            if j >= 1:
+                sum_exps_chunk(j - 1)
+            if j == 1:
+                z_tiles = psum_t.tile([P, LATENT_TILES, P], F32, tag="t")
+                for t in range(LATENT_TILES):
+                    nc.tensor.transpose(z_tiles[:, t, :], zT[:, t, :], identity[:])
+                z_rows = keep.tile([P, LATENT], F32)
+                nc.scalar.copy(
+                    out=z_rows[:].rearrange("b (q t) -> b q t", t=PACK),
+                    in_=z_tiles[:].rearrange("b t q -> b q t"),
+                )
+                nc.sync.dma_start(out=z_out, in_=z_rows[:])
+        sum_exps_chunk(CHUNKS - 1)
+
+        log_sum = keep.tile([P, MODULES], F32)
+        nc.scalar.activation(out=log_sum[:], in_=exp_sum[:], func=ACT.Ln)
+        conf = keep.tile([P, MODULES], F32)
+        nc.vector.tensor_sub(out=conf[:], in0=neg_max[:], in1=log_sum[:])
+        nc.sync.dma_start(out=conf_out, in_=conf[:])

@@ -28,6 +28,7 @@ CHUNKS = MODULES * HEADS // CHUNK_ROWS
 ROWS_PER_PARTITION = CHUNK_ROWS // P
 CHUNK_MODULES = CHUNK_ROWS // HEADS
 GROUP_MODULES = CHUNK_MODULES // 2
+VECTOR_Q = 96
 
 FLOPS = 2 * P * HIDDEN * LATENT + 2 * P * LATENT * MODULES * HEADS
 
@@ -36,12 +37,13 @@ def tile_ace_pa_s_kernel(tc, h_enc, enc_w2, enc_b2, clus_w, clus_b, z_out, conf_
     nc = tc.nc
     with ExitStack() as stack:
         keep = stack.enter_context(tc.tile_pool(name="keep", bufs=1))
-        psum_t = stack.enter_context(tc.psum_pool(name="psum_t", bufs=4))
-        psum_mx = stack.enter_context(tc.psum_pool(name="psum_mx", bufs=4))
+        psum_t = stack.enter_context(tc.psum_pool(name="psum_t", bufs=5))
+        psum_mx = stack.enter_context(tc.psum_pool(name="psum_mx", bufs=3))
+        stack.enter_context(tc.manual_schedule())
 
-        cb_bf16 = keep.tile([P, CHUNKS, ROWS_PER_PARTITION], BF16)
+        cb = keep.tile([P, CHUNKS, ROWS_PER_PARTITION], BF16)
         nc.sync.dma_start(
-            out=cb_bf16[:],
+            out=cb[:],
             in_=clus_b.rearrange("c k -> (c k)").rearrange(
                 "(j p r) -> p j r", j=CHUNKS, r=ROWS_PER_PARTITION
             ),
@@ -56,11 +58,8 @@ def tile_ace_pa_s_kernel(tc, h_enc, enc_w2, enc_b2, clus_w, clus_b, z_out, conf_
             w2_rows.append(rows)
         h_rows = keep.tile([P, HIDDEN], BF16)
         nc.sync.dma_start(out=h_rows[:], in_=h_enc)
-        b2_bf16 = keep.tile([P, PACK], BF16)
-        nc.sync.dma_start(
-            out=b2_bf16[:],
-            in_=enc_b2.rearrange("(q t) -> q t", t=PACK),
-        )
+        b2 = keep.tile([P, PACK], BF16)
+        nc.sync.dma_start(out=b2[:], in_=enc_b2.rearrange("(q t) -> q t", t=PACK))
         clus_w_rows = clus_w.rearrange("c k d -> (c k) d")
         cw_rows = []
         for j in range(CHUNKS):
@@ -72,6 +71,8 @@ def tile_ace_pa_s_kernel(tc, h_enc, enc_w2, enc_b2, clus_w, clus_b, z_out, conf_
                 ),
             )
             cw_rows.append(rows)
+        b2_rows = keep.tile([P, LATENT], BF16)
+        nc.sync.dma_start(out=b2_rows[:], in_=enc_b2.partition_broadcast(P))
 
         identity = keep.tile([P, P], F32)
         make_identity(nc, identity[:])
@@ -79,54 +80,26 @@ def tile_ace_pa_s_kernel(tc, h_enc, enc_w2, enc_b2, clus_w, clus_b, z_out, conf_
         nc.vector.memset(one_column[:], 0.0)
         table_warmer = keep.tile([P, 1], F32)
         nc.scalar.activation(out=table_warmer[:], in_=one_column[:], func=ACT.Exp)
+        identity_bf16 = keep.tile([P, P], BF16)
+        nc.vector.tensor_copy(out=identity_bf16[:], in_=identity[:])
 
-        cb_scaled = keep.tile([P, CHUNKS, ROWS_PER_PARTITION], F32)
-        nc.vector.tensor_scalar_mul(out=cb_scaled[:], in0=cb_bf16[:], scalar1=-BETA)
-        bias_rows = []
-        for j in range(CHUNKS):
-            spread = psum_t.tile([P, ROWS_PER_PARTITION, P], F32, tag="t")
-            for r in range(ROWS_PER_PARTITION):
-                nc.tensor.transpose(
-                    spread[:, r, :], cb_scaled[:, j, r : r + 1].to_broadcast([P, P]), identity[:]
-                )
-            rows = keep.tile([P, CHUNK_ROWS], F32, name="bias_rows%d" % j)
-            nc.scalar.copy(out=rows[:], in_=spread[:].rearrange("b r p -> b (r p)"))
-            bias_rows.append(rows)
-
-        w2_grouped = []
-        for g in range(HIDDEN_PASSES):
-            grouped = keep.tile([P, LATENT * PACK], BF16, align_bytes=64, name="w2_grouped%d" % g)
-            nc.vector.tensor_copy(
-                out=grouped[:].rearrange("p (t q j) -> p t q j", t=PACK, j=PACK),
-                in_=w2_rows[g][:].rearrange("p j (q t) -> p t q j", t=PACK),
-            )
-            w2_grouped.append(grouped)
-        w2_codes = []
-        w2_scales = []
-        for g in range(HIDDEN_PASSES):
-            codes = keep.tile([P, LATENT], U32, align_bytes=64, name="w2_codes%d" % g)
-            scales = keep.tile([P, LATENT], U8, align_bytes=64, name="w2_scales%d" % g)
-            nc.vector.quantize_mx(out=codes[:].bitcast(FP8X4), scales=scales[:], in_=w2_grouped[g][:])
-            w2_codes.append(codes)
-            w2_scales.append(scales)
-
-        h_words = h_rows[:].bitcast(F32)
-        h_wordsT = psum_t.tile([P, HIDDEN_PASSES, 2, P], F32, tag="t")
-        for g in range(HIDDEN_PASSES):
-            for u in range(2):
-                every_2nd = slice(2 * g * P + u, 2 * (g + 1) * P, 2)
-                nc.tensor.transpose(h_wordsT[:, g, u, :], h_words[:, every_2nd], identity[:])
+        bias_rows = [keep.tile([P, CHUNK_ROWS], F32, name="bias_rows%d" % j) for j in range(CHUNKS)]
+        w2_grouped = [
+            keep.tile([P, LATENT * PACK], BF16, align_bytes=64, name="w2_grouped%d" % g)
+            for g in range(HIDDEN_PASSES)
+        ]
+        w2_codes = [
+            keep.tile([P, LATENT], U32, align_bytes=64, name="w2_codes%d" % g) for g in range(HIDDEN_PASSES)
+        ]
+        w2_scales = [
+            keep.tile([P, LATENT], U8, align_bytes=64, name="w2_scales%d" % g) for g in range(HIDDEN_PASSES)
+        ]
         h_grouped = keep.tile([P, HIDDEN_PASSES * P * PACK], BF16, align_bytes=64)
-        nc.scalar.copy(
-            out=h_grouped[:].bitcast(F32).rearrange("q (g b u) -> q g b u", g=HIDDEN_PASSES, u=2),
-            in_=h_wordsT[:].rearrange("q g u b -> q g b u"),
-        )
-        b2 = keep.tile([P, PACK], F32)
-        nc.vector.tensor_copy(out=b2[:], in_=b2_bf16[:])
         h_codes = keep.tile([P, HIDDEN_PASSES * P], U32, align_bytes=64)
         h_scales = keep.tile([P, HIDDEN_PASSES * P], U8, align_bytes=64)
-        nc.vector.quantize_mx(out=h_codes[:].bitcast(FP8X4), scales=h_scales[:], in_=h_grouped[:])
-
+        z_grouped = keep.tile([P, P * PACK], BF16, align_bytes=64)
+        z_codes = keep.tile([P, P], U32, align_bytes=64)
+        z_scales = keep.tile([P, P], U8, align_bytes=64)
         cw_grouped = [
             keep.tile([P, CHUNK_ROWS * PACK], BF16, align_bytes=64, name="cw_grouped%d" % j)
             for j in range(CHUNKS)
@@ -141,36 +114,72 @@ def tile_ace_pa_s_kernel(tc, h_enc, enc_w2, enc_b2, clus_w, clus_b, z_out, conf_
         neg_max = keep.tile([P, MODULES], F32)
         exp_sum = keep.tile([P, MODULES], F32)
 
+        def spread_bias(j):
+            spread = psum_t.tile([P, ROWS_PER_PARTITION, P], BF16, name="spread", tag="t")
+            for r in range(ROWS_PER_PARTITION):
+                nc.tensor.transpose(
+                    spread[:, r, :], cb[:, j, r : r + 1].to_broadcast([P, P]), identity_bf16[:]
+                )
+            return spread[:].rearrange("b r p -> b (r p)")
+
+        def scale_bias_scalar(j):
+            nc.scalar.activation(out=bias_rows[j][:], in_=spreads[j], func=ACT.Copy, scale=-BETA)
+
+        def scale_bias_vector(j):
+            nc.vector.tensor_scalar_mul(out=bias_rows[j][:], in0=spreads[j], scalar1=-BETA)
+
+        def regroup_w2(g):
+            to = w2_grouped[g][:].rearrange("p (t q j) -> p t q j", t=PACK, j=PACK)
+            of = w2_rows[g][:].rearrange("p j (q t) -> p t q j", t=PACK)
+            nc.vector.tensor_copy(out=to[:, :, :VECTOR_Q, :], in_=of[:, :, :VECTOR_Q, :])
+            nc.scalar.copy(out=to[:, :, VECTOR_Q:, :], in_=of[:, :, VECTOR_Q:, :])
+
+        def quantise(codes, scales, grouped):
+            nc.vector.quantize_mx(out=codes[:].bitcast(FP8X4), scales=scales[:], in_=grouped[:])
+
+        def transpose_h():
+            h_words = h_rows[:].bitcast(F32)
+            wordsT = psum_t.tile([P, HIDDEN_PASSES, 2, P], F32, name="h_wordsT", tag="t")
+            for g in range(HIDDEN_PASSES):
+                for u in range(2):
+                    every_2nd = slice(2 * g * P + u, 2 * (g + 1) * P, 2)
+                    nc.tensor.transpose(wordsT[:, g, u, :], h_words[:, every_2nd], identity[:])
+            return wordsT
+
         def by_module(columns):
             return columns.rearrange("b (r m i) -> b m r i", r=ROWS_PER_PARTITION, m=CHUNK_MODULES)
 
         def by_row(columns):
             return columns.rearrange("b (r m i) -> b r m i", r=ROWS_PER_PARTITION, m=CHUNK_MODULES)
 
-        def transpose_chunk(j):
+        def transpose_half(j, half):
             words = cw_rows[j][:].bitcast(F32)
+            wordsT = psum_t.tile([P, 2, 2, P], F32, name="cw_wordsT", tag="t")
+            for r in range(2):
+                for u in range(2):
+                    row = 2 * half + r
+                    every_2nd = slice(2 * row * P + u, 2 * (row + 1) * P, 2)
+                    nc.tensor.transpose(wordsT[:, r, u, :], words[:, every_2nd], identity[:])
+            return wordsT
+
+        def transpose_chunk(j):
+            return [transpose_half(j, half) for half in range(2)]
+
+        def regroup_chunk(j, halves):
             grouped_words = cw_grouped[j][:].bitcast(F32).rearrange(
                 "q (r p u) -> q r p u", r=ROWS_PER_PARTITION, u=2
             )
             for half in range(2):
-                wordsT = psum_t.tile([P, 2, 2, P], F32, tag="t")
-                for r in range(2):
-                    for u in range(2):
-                        row = 2 * half + r
-                        every_2nd = slice(2 * row * P + u, 2 * (row + 1) * P, 2)
-                        nc.tensor.transpose(wordsT[:, r, u, :], words[:, every_2nd], identity[:])
                 nc.scalar.copy(
                     out=grouped_words[:, 2 * half : 2 * half + 2, :, :],
-                    in_=wordsT[:].rearrange("q r u p -> q r p u"),
+                    in_=halves[half][:].rearrange("q r u p -> q r p u"),
                 )
 
         def quantise_chunk(j):
-            nc.vector.quantize_mx(
-                out=cw_codes[j][:].bitcast(FP8X4), scales=cw_scales[j][:], in_=cw_grouped[j][:]
-            )
+            quantise(cw_codes[j], cw_scales[j], cw_grouped[j])
 
-        def score_chunk(j):
-            sums = psum_mx.tile([P, CHUNK_ROWS], F32, tag="mx")
+        def multiply_chunk(j):
+            sums = psum_mx.tile([P, CHUNK_ROWS], F32, name="sums", tag="mx")
             nc.tensor.matmul_mx(
                 out=sums[:],
                 lhsT=z_codes[:].bitcast(FP8X4),
@@ -180,8 +189,15 @@ def tile_ace_pa_s_kernel(tc, h_enc, enc_w2, enc_b2, clus_w, clus_b, z_out, conf_
                 start=True,
                 stop=True,
             )
-            for first in range(0, CHUNK_MODULES, GROUP_MODULES):
-                group = slice(first, first + GROUP_MODULES)
+            return sums
+
+        def groups_of(j):
+            modules = CHUNK_MODULES if j < CHUNKS - 2 else GROUP_MODULES
+            return [(first, modules) for first in range(0, CHUNK_MODULES, modules)]
+
+        def scale_chunk(j, sums):
+            for first, modules in groups_of(j):
+                group = slice(first, first + modules)
                 nc.vector.scalar_tensor_tensor(
                     out=by_row(scaled[j][:])[:, :, group, :].rearrange("b r m i -> b r (m i)"),
                     in0=by_row(sums[:])[:, :, group, :].rearrange("b r m i -> b r (m i)"),
@@ -190,11 +206,13 @@ def tile_ace_pa_s_kernel(tc, h_enc, enc_w2, enc_b2, clus_w, clus_b, z_out, conf_
                     op0=ALU.mult,
                     op1=ALU.add,
                 )
-            for first in range(0, CHUNK_MODULES, GROUP_MODULES):
+
+        def max_chunk(j):
+            for first, modules in groups_of(j):
                 c = j * CHUNK_MODULES + first
                 nc.vector.tensor_reduce(
-                    out=neg_max[:, c : c + GROUP_MODULES],
-                    in_=by_module(scaled[j][:])[:, first : first + GROUP_MODULES, :, :],
+                    out=neg_max[:, c : c + modules],
+                    in_=by_module(scaled[j][:])[:, first : first + modules, :, :],
                     axis=AXIS.XY,
                     op=ALU.max,
                     negate=True,
@@ -212,9 +230,24 @@ def tile_ace_pa_s_kernel(tc, h_enc, enc_w2, enc_b2, clus_w, clus_b, z_out, conf_
                     accum_out=exp_sum[:, c : c + 1],
                 )
 
-        transpose_chunk(0)
+        spreads = [spread_bias(j) for j in range(CHUNKS)]
+        regroup_w2(0)
+        scale_bias_scalar(0)
+        quantise(w2_codes[0], w2_scales[0], w2_grouped[0])
+        h_wordsT = transpose_h()
+        regroup_w2(1)
+        scale_bias_scalar(1)
+        quantise(w2_codes[1], w2_scales[1], w2_grouped[1])
+        nc.scalar.copy(
+            out=h_grouped[:].bitcast(F32).rearrange("q (g b u) -> q g b u", g=HIDDEN_PASSES, u=2),
+            in_=h_wordsT[:].rearrange("q g u b -> q g b u"),
+        )
+        quantise(h_codes, h_scales, h_grouped)
+        halves0 = transpose_chunk(0)
+        scale_bias_vector(2)
+        scale_bias_vector(3)
 
-        zT_sums = psum_mx.tile([P, LATENT_TILES, P], F32, tag="mx")
+        zT_sums = psum_mx.tile([P, LATENT_TILES, P], F32, name="zT_sums", tag="mx")
         for t in range(LATENT_TILES):
             for g in range(HIDDEN_PASSES):
                 nc.tensor.matmul_mx(
@@ -226,47 +259,61 @@ def tile_ace_pa_s_kernel(tc, h_enc, enc_w2, enc_b2, clus_w, clus_b, z_out, conf_
                     start=(g == 0),
                     stop=(g == HIDDEN_PASSES - 1),
                 )
-
-        transpose_chunk(1)
-
-        z_grouped = keep.tile([P, P * PACK], BF16, align_bytes=64)
+        regroup_chunk(0, halves0)
         nc.vector.tensor_tensor(
             out=z_grouped[:].rearrange("q (b t) -> q b t", t=PACK),
             in0=zT_sums[:].rearrange("q t b -> q b t"),
             in1=b2[:].unsqueeze(1).to_broadcast([P, P, PACK]),
             op=ALU.add,
         )
+        halves1 = transpose_chunk(1)
         quantise_chunk(0)
-        z_codes = keep.tile([P, P], U32, align_bytes=64)
-        z_scales = keep.tile([P, P], U8, align_bytes=64)
-        nc.vector.quantize_mx(out=z_codes[:].bitcast(FP8X4), scales=z_scales[:], in_=z_grouped[:])
+        quantise(z_codes, z_scales, z_grouped)
+        regroup_chunk(1, halves1)
+        halves2 = transpose_chunk(2)
         quantise_chunk(1)
 
-        zT = keep.tile([P, LATENT_TILES, P], F32)
-        for t in range(LATENT_TILES):
-            nc.scalar.activation(
-                out=zT[:, t, :], in_=zT_sums[:, t, :], func=ACT.Identity, bias=b2[:, t : t + 1]
+        sums0 = multiply_chunk(0)
+        regroup_chunk(2, halves2)
+        halves3 = transpose_chunk(3)
+        scale_chunk(0, sums0)
+        sums1 = multiply_chunk(1)
+        quantise_chunk(2)
+        max_chunk(0)
+        regroup_chunk(3, halves3)
+        sum_exps_chunk(0)
+        scale_chunk(1, sums1)
+        sums2 = multiply_chunk(2)
+        quantise_chunk(3)
+        max_chunk(1)
+        sum_exps_chunk(1)
+        scale_chunk(2, sums2)
+        sums3 = multiply_chunk(3)
+        max_chunk(2)
+        sum_exps_chunk(2)
+        scale_chunk(3, sums3)
+        z_sums = psum_mx.tile([P, LATENT_TILES, P], F32, name="z_sums", tag="mx")
+        for g in range(HIDDEN_PASSES):
+            nc.tensor.matmul_mx(
+                out=z_sums[:].rearrange("b t q -> b (t q)"),
+                lhsT=h_codes[:, g * P : (g + 1) * P].bitcast(FP8X4),
+                lhsT_scale=h_scales[:, g * P : (g + 1) * P],
+                rhs=w2_codes[g][:].bitcast(FP8X4),
+                rhs_scale=w2_scales[g][:],
+                start=(g == 0),
+                stop=(g == HIDDEN_PASSES - 1),
             )
+        max_chunk(3)
+        sum_exps_chunk(3)
 
-        for j in range(CHUNKS):
-            if j + 2 < CHUNKS:
-                transpose_chunk(j + 2)
-            score_chunk(j)
-            if j + 2 < CHUNKS:
-                quantise_chunk(j + 2)
-            if j >= 1:
-                sum_exps_chunk(j - 1)
-            if j == 1:
-                z_tiles = psum_t.tile([P, LATENT_TILES, P], F32, tag="t")
-                for t in range(LATENT_TILES):
-                    nc.tensor.transpose(z_tiles[:, t, :], zT[:, t, :], identity[:])
-                z_rows = keep.tile([P, LATENT], F32)
-                nc.scalar.copy(
-                    out=z_rows[:].rearrange("b (q t) -> b q t", t=PACK),
-                    in_=z_tiles[:].rearrange("b t q -> b q t"),
-                )
-                nc.sync.dma_start(out=z_out, in_=z_rows[:])
-        sum_exps_chunk(CHUNKS - 1)
+        z_rows = keep.tile([P, LATENT], F32)
+        nc.vector.tensor_tensor(
+            out=z_rows[:].rearrange("b (q t) -> b q t", t=PACK),
+            in0=z_sums[:].rearrange("b t q -> b q t"),
+            in1=b2_rows[:].rearrange("b (q t) -> b q t", t=PACK),
+            op=ALU.add,
+        )
+        nc.sync.dma_start(out=z_out, in_=z_rows[:])
 
         log_sum = keep.tile([P, MODULES], F32)
         nc.scalar.activation(out=log_sum[:], in_=exp_sum[:], func=ACT.Ln)

@@ -243,6 +243,17 @@ def tile_ace_pa_s_kernel(tc, h_enc, enc_w2, enc_b2, clus_w, clus_b, z_out, conf_
             in_=h_wordsT[:].rearrange("q g u b -> q g b u"),
         )
         quantise(h_codes, h_scales, h_grouped)
+        unread = psum_mx.tile([P, LATENT], F32, name="unread", tag="mx")
+        for warm in range(3):
+            nc.tensor.matmul_mx(
+                out=unread[:],
+                lhsT=w2_codes[0][:, :P].bitcast(FP8X4),
+                lhsT_scale=w2_scales[0][:, :P],
+                rhs=w2_codes[0][:].bitcast(FP8X4),
+                rhs_scale=w2_scales[0][:],
+                start=True,
+                stop=True,
+            )
         halves0 = transpose_chunk(0)
         scale_bias_vector(2)
         scale_bias_vector(3)

@@ -27,6 +27,7 @@ CHUNK_ROWS = 512
 CHUNKS = MODULES * HEADS // CHUNK_ROWS
 ROWS_PER_PARTITION = CHUNK_ROWS // P
 CHUNK_MODULES = CHUNK_ROWS // HEADS
+SLOTS = 16
 GROUP_MODULES = CHUNK_MODULES // 2
 VECTOR_Q = 96
 
@@ -41,12 +42,9 @@ def tile_ace_pa_s_kernel(tc, h_enc, enc_w2, enc_b2, clus_w, clus_b, z_out, conf_
         psum_mx = stack.enter_context(tc.psum_pool(name="psum_mx", bufs=3))
         stack.enter_context(tc.manual_schedule())
 
-        cb = keep.tile([P, CHUNKS, ROWS_PER_PARTITION], BF16)
+        cb = keep.tile([P, SLOTS], BF16)
         nc.sync.dma_start(
-            out=cb[:],
-            in_=clus_b.rearrange("c k -> (c k)").rearrange(
-                "(j p r) -> p j r", j=CHUNKS, r=ROWS_PER_PARTITION
-            ),
+            out=cb[:], in_=clus_b.rearrange("c k -> (c k)").rearrange("(p r) -> p r", r=SLOTS)
         )
         w2_rows = []
         for g in range(HIDDEN_PASSES):
@@ -56,21 +54,21 @@ def tile_ace_pa_s_kernel(tc, h_enc, enc_w2, enc_b2, clus_w, clus_b, z_out, conf_
                 in_=enc_w2[g * K_PASS : (g + 1) * K_PASS, :].rearrange("(q t) d -> q t d", t=PACK),
             )
             w2_rows.append(rows)
-        h_rows = keep.tile([P, HIDDEN], BF16)
-        nc.sync.dma_start(out=h_rows[:], in_=h_enc)
+            if g == 0:
+                h_rows = keep.tile([P, HIDDEN], BF16)
+                nc.sync.dma_start(out=h_rows[:], in_=h_enc)
         b2 = keep.tile([P, PACK], BF16)
         nc.sync.dma_start(out=b2[:], in_=enc_b2.rearrange("(q t) -> q t", t=PACK))
         clus_w_rows = clus_w.rearrange("c k d -> (c k) d")
         cw_rows = []
         for j in range(CHUNKS):
-            rows = keep.tile([P, ROWS_PER_PARTITION * LATENT], BF16, name="cw_rows%d" % j)
-            nc.sync.dma_start(
-                out=rows[:],
-                in_=clus_w_rows[j * CHUNK_ROWS : (j + 1) * CHUNK_ROWS, :].rearrange(
-                    "(p r) d -> p (r d)", r=ROWS_PER_PARTITION
-                ),
+            halves = clus_w_rows[j * CHUNK_ROWS : (j + 1) * CHUNK_ROWS, :].rearrange(
+                "(p h r) d -> h p (r d)", h=2, r=2
             )
-            cw_rows.append(rows)
+            for h in range(2):
+                rows = keep.tile([P, 2 * LATENT], BF16, name="cw_rows%d_%d" % (j, h))
+                nc.sync.dma_start(out=rows[:], in_=halves[h])
+                cw_rows.append(rows)
         b2_rows = keep.tile([P, LATENT], BF16)
         nc.sync.dma_start(out=b2_rows[:], in_=enc_b2.partition_broadcast(P))
 
@@ -82,8 +80,13 @@ def tile_ace_pa_s_kernel(tc, h_enc, enc_w2, enc_b2, clus_w, clus_b, z_out, conf_
         nc.scalar.activation(out=table_warmer[:], in_=one_column[:], func=ACT.Exp)
         identity_bf16 = keep.tile([P, P], BF16)
         nc.vector.tensor_copy(out=identity_bf16[:], in_=identity[:])
+        permutation = keep.tile([P, P], F32)
+        nc.vector.tensor_copy(
+            out=permutation[:].rearrange("k (o i) -> k o i", o=4),
+            in_=identity[:].rearrange("k (i o) -> k o i", o=4),
+        )
 
-        bias_rows = [keep.tile([P, CHUNK_ROWS], F32, name="bias_rows%d" % j) for j in range(CHUNKS)]
+        bias_rows = keep.tile([P, SLOTS, P], F32)
         w2_grouped = [
             keep.tile([P, LATENT * PACK], BF16, align_bytes=64, name="w2_grouped%d" % g)
             for g in range(HIDDEN_PASSES)
@@ -114,28 +117,39 @@ def tile_ace_pa_s_kernel(tc, h_enc, enc_w2, enc_b2, clus_w, clus_b, z_out, conf_
         neg_max = keep.tile([P, MODULES], F32)
         exp_sum = keep.tile([P, MODULES], F32)
 
-        def spread_bias(j):
-            spread = psum_t.tile([P, ROWS_PER_PARTITION, P], BF16, name="spread", tag="t")
-            for r in range(ROWS_PER_PARTITION):
+        def spread_bias(first):
+            spread = psum_t.tile([P, SLOTS // 2, P], BF16, name="spread", tag="t")
+            for s in range(SLOTS // 2):
+                r, o = divmod(first + s, 4)
+                column = 4 * o + r
                 nc.tensor.transpose(
-                    spread[:, r, :], cb[:, j, r : r + 1].to_broadcast([P, P]), identity_bf16[:]
+                    spread[:, s, :], cb[:, column : column + 1].to_broadcast([P, P]), identity_bf16[:]
                 )
-            return spread[:].rearrange("b r p -> b (r p)")
+            return spread
 
-        def scale_bias_scalar(j):
-            nc.scalar.activation(out=bias_rows[j][:], in_=spreads[j], func=ACT.Copy, scale=-BETA)
+        def scale_bias_scalar(to, of):
+            nc.scalar.activation(out=to, in_=of, func=ACT.Copy, scale=-BETA)
 
-        def scale_bias_vector(j):
-            nc.vector.tensor_scalar_mul(out=bias_rows[j][:], in0=spreads[j], scalar1=-BETA)
+        def scale_bias_vector(to, of):
+            nc.vector.tensor_scalar_mul(out=to, in0=of, scalar1=-BETA)
 
-        def regroup_w2(g):
+        def regroup_w2(g, first, tiles):
             to = w2_grouped[g][:].rearrange("p (t q j) -> p t q j", t=PACK, j=PACK)
             of = w2_rows[g][:].rearrange("p j (q t) -> p t q j", t=PACK)
+            to, of = to[:, first : first + tiles, :, :], of[:, first : first + tiles, :, :]
             nc.vector.tensor_copy(out=to[:, :, :VECTOR_Q, :], in_=of[:, :, :VECTOR_Q, :])
             nc.scalar.copy(out=to[:, :, VECTOR_Q:, :], in_=of[:, :, VECTOR_Q:, :])
 
         def quantise(codes, scales, grouped):
-            nc.vector.quantize_mx(out=codes[:].bitcast(FP8X4), scales=scales[:], in_=grouped[:])
+            nc.vector.quantize_mx(out=codes.bitcast(FP8X4), scales=scales, in_=grouped)
+
+        def quantise_w2(g, first, tiles):
+            columns = slice(first * P, (first + tiles) * P)
+            quantise(
+                w2_codes[g][:, columns],
+                w2_scales[g][:, columns],
+                w2_grouped[g][:, first * P * PACK : (first + tiles) * P * PACK],
+            )
 
         def transpose_h():
             h_words = h_rows[:].bitcast(F32)
@@ -147,19 +161,19 @@ def tile_ace_pa_s_kernel(tc, h_enc, enc_w2, enc_b2, clus_w, clus_b, z_out, conf_
             return wordsT
 
         def by_module(columns):
-            return columns.rearrange("b (r m i) -> b m r i", r=ROWS_PER_PARTITION, m=CHUNK_MODULES)
+            return columns.rearrange("b (s m i) -> b m s i", s=SLOTS, m=CHUNK_MODULES)
 
-        def by_row(columns):
-            return columns.rearrange("b (r m i) -> b r m i", r=ROWS_PER_PARTITION, m=CHUNK_MODULES)
+        def by_slot(columns, first, modules):
+            columns = columns.rearrange("b (s m i) -> b s m i", s=SLOTS, m=CHUNK_MODULES)
+            return columns[:, :, first : first + modules, :].rearrange("b s m i -> b s (m i)")
 
         def transpose_half(j, half):
-            words = cw_rows[j][:].bitcast(F32)
+            words = cw_rows[2 * j + half][:].bitcast(F32)
             wordsT = psum_t.tile([P, 2, 2, P], F32, name="cw_wordsT", tag="t")
             for r in range(2):
                 for u in range(2):
-                    row = 2 * half + r
-                    every_2nd = slice(2 * row * P + u, 2 * (row + 1) * P, 2)
-                    nc.tensor.transpose(wordsT[:, r, u, :], words[:, every_2nd], identity[:])
+                    every_2nd = slice(2 * r * P + u, 2 * (r + 1) * P, 2)
+                    nc.tensor.transpose(wordsT[:, r, u, :], words[:, every_2nd], permutation[:])
             return wordsT
 
         def transpose_chunk(j):
@@ -176,7 +190,7 @@ def tile_ace_pa_s_kernel(tc, h_enc, enc_w2, enc_b2, clus_w, clus_b, z_out, conf_
                 )
 
         def quantise_chunk(j):
-            quantise(cw_codes[j], cw_scales[j], cw_grouped[j])
+            quantise(cw_codes[j][:], cw_scales[j][:], cw_grouped[j][:])
 
         def multiply_chunk(j):
             sums = psum_mx.tile([P, CHUNK_ROWS], F32, name="sums", tag="mx")
@@ -197,12 +211,12 @@ def tile_ace_pa_s_kernel(tc, h_enc, enc_w2, enc_b2, clus_w, clus_b, z_out, conf_
 
         def scale_chunk(j, sums):
             for first, modules in groups_of(j):
-                group = slice(first, first + modules)
+                p = 32 * j + 4 * first
                 nc.vector.scalar_tensor_tensor(
-                    out=by_row(scaled[j][:])[:, :, group, :].rearrange("b r m i -> b r (m i)"),
-                    in0=by_row(sums[:])[:, :, group, :].rearrange("b r m i -> b r (m i)"),
+                    out=by_slot(scaled[j][:], first, modules),
+                    in0=by_slot(sums[:], first, modules),
                     scalar=-BETA,
-                    in1=by_row(bias_rows[j][:])[:, :, group, :].rearrange("b r m i -> b r (m i)"),
+                    in1=bias_rows[:, :, p : p + 4 * modules],
                     op0=ALU.mult,
                     op1=ALU.add,
                 )
@@ -230,21 +244,23 @@ def tile_ace_pa_s_kernel(tc, h_enc, enc_w2, enc_b2, clus_w, clus_b, z_out, conf_
                     accum_out=exp_sum[:, c : c + 1],
                 )
 
-        spreads = [spread_bias(j) for j in range(CHUNKS)]
-        regroup_w2(0)
-        scale_bias_scalar(0)
-        quantise(w2_codes[0], w2_scales[0], w2_grouped[0])
+        spread0 = spread_bias(0)
+        spread1 = spread_bias(SLOTS // 2)
+        regroup_w2(0, 0, LATENT_TILES)
+        scale_bias_scalar(bias_rows[:, : SLOTS // 2, :], spread0[:])
+        quantise_w2(0, 0, LATENT_TILES)
         h_wordsT = transpose_h()
-        regroup_w2(1)
-        scale_bias_scalar(1)
-        quantise(w2_codes[1], w2_scales[1], w2_grouped[1])
         nc.scalar.copy(
             out=h_grouped[:].bitcast(F32).rearrange("q (g b u) -> q g b u", g=HIDDEN_PASSES, u=2),
             in_=h_wordsT[:].rearrange("q g u b -> q g b u"),
         )
-        quantise(h_codes, h_scales, h_grouped)
+        regroup_w2(1, 0, 2)
+        regroup_w2(1, 2, 2)
+        quantise(h_codes[:], h_scales[:], h_grouped[:])
+        quantise_w2(1, 0, 2)
+        quantise_w2(1, 2, 2)
         unread = psum_mx.tile([P, LATENT], F32, name="unread", tag="mx")
-        for warm in range(3):
+        for warm in range(2):
             nc.tensor.matmul_mx(
                 out=unread[:],
                 lhsT=w2_codes[0][:, :P].bitcast(FP8X4),
@@ -255,8 +271,8 @@ def tile_ace_pa_s_kernel(tc, h_enc, enc_w2, enc_b2, clus_w, clus_b, z_out, conf_
                 stop=True,
             )
         halves0 = transpose_chunk(0)
-        scale_bias_vector(2)
-        scale_bias_vector(3)
+        scale_bias_scalar(bias_rows[:, SLOTS // 2 : 3 * SLOTS // 4, :], spread1[:, : SLOTS // 4, :])
+        scale_bias_vector(bias_rows[:, 3 * SLOTS // 4 :, :], spread1[:, SLOTS // 4 :, :])
 
         zT_sums = psum_mx.tile([P, LATENT_TILES, P], F32, name="zT_sums", tag="mx")
         for t in range(LATENT_TILES):
@@ -279,7 +295,7 @@ def tile_ace_pa_s_kernel(tc, h_enc, enc_w2, enc_b2, clus_w, clus_b, z_out, conf_
         )
         halves1 = transpose_chunk(1)
         quantise_chunk(0)
-        quantise(z_codes, z_scales, z_grouped)
+        quantise(z_codes[:], z_scales[:], z_grouped[:])
         regroup_chunk(1, halves1)
         halves2 = transpose_chunk(2)
         quantise_chunk(1)

@@ -244,6 +244,11 @@ def tile_ace_pa_s_kernel(tc, h_enc, enc_w2, enc_b2, clus_w, clus_b, z_out, conf_
                     accum_out=exp_sum[:, c : c + 1],
                 )
 
+        zeros = keep.tile([P, LATENT], F32)
+        nc.vector.memset(zeros[:], 0.0)
+        unread = psum_mx.tile([P, LATENT], F32, name="unread", tag="mx")
+        nc.tensor.matmul(unread[:], lhsT=zeros[:, :P], rhs=zeros[:], start=True, stop=True)
+
         spread0 = spread_bias(0)
         spread1 = spread_bias(SLOTS // 2)
         regroup_w2(0, 0, LATENT_TILES)
@@ -259,8 +264,7 @@ def tile_ace_pa_s_kernel(tc, h_enc, enc_w2, enc_b2, clus_w, clus_b, z_out, conf_
         quantise(h_codes[:], h_scales[:], h_grouped[:])
         quantise_w2(1, 0, 2)
         quantise_w2(1, 2, 2)
-        unread = psum_mx.tile([P, LATENT], F32, name="unread", tag="mx")
-        for warm in range(2):
+        for warm in range(3):
             nc.tensor.matmul_mx(
                 out=unread[:],
                 lhsT=w2_codes[0][:, :P].bitcast(FP8X4),

@@ -74,10 +74,18 @@ def tile_ace_pa_s_kernel(tc, h_enc, enc_w2, enc_b2, clus_w, clus_b, z_out, conf_
 
         identity = keep.tile([P, P], F32)
         make_identity(nc, identity[:])
-        one_column = keep.tile([P, 1], F32)
-        nc.vector.memset(one_column[:], 0.0)
+        zeros = keep.tile([P, P], F32)
+        nc.vector.memset(zeros[:], 0.0)
         table_warmer = keep.tile([P, 1], F32)
-        nc.scalar.activation(out=table_warmer[:], in_=one_column[:], func=ACT.Exp)
+        nc.scalar.activation(out=table_warmer[:], in_=zeros[:, :1], func=ACT.Exp)
+        unread = psum_mx.tile([P, LATENT], F32, name="unread", tag="mx")
+        nc.tensor.matmul(
+            unread[:].rearrange("p (n c) -> p n c", c=P),
+            lhsT=zeros[:],
+            rhs=zeros[:].unsqueeze(1).to_broadcast([P, LATENT_TILES, P]),
+            start=True,
+            stop=True,
+        )
         identity_bf16 = keep.tile([P, P], BF16)
         nc.vector.tensor_copy(out=identity_bf16[:], in_=identity[:])
         permutation = keep.tile([P, P], F32)
@@ -244,11 +252,6 @@ def tile_ace_pa_s_kernel(tc, h_enc, enc_w2, enc_b2, clus_w, clus_b, z_out, conf_
                     accum_out=exp_sum[:, c : c + 1],
                 )
 
-        zeros = keep.tile([P, LATENT], F32)
-        nc.vector.memset(zeros[:], 0.0)
-        unread = psum_mx.tile([P, LATENT], F32, name="unread", tag="mx")
-        nc.tensor.matmul(unread[:], lhsT=zeros[:, :P], rhs=zeros[:], start=True, stop=True)
-
         spread0 = spread_bias(0)
         spread1 = spread_bias(SLOTS // 2)
         regroup_w2(0, 0, LATENT_TILES)
@@ -264,7 +267,7 @@ def tile_ace_pa_s_kernel(tc, h_enc, enc_w2, enc_b2, clus_w, clus_b, z_out, conf_
         quantise(h_codes[:], h_scales[:], h_grouped[:])
         quantise_w2(1, 0, 2)
         quantise_w2(1, 2, 2)
-        for warm in range(3):
+        for warm in range(2):
             nc.tensor.matmul_mx(
                 out=unread[:],
                 lhsT=w2_codes[0][:, :P].bitcast(FP8X4),

@@ -142,11 +142,14 @@ def tile_ace_pa_s_kernel(tc, h_enc, enc_w2, enc_b2, clus_w, clus_b, z_out, conf_
             nc.vector.tensor_scalar_mul(out=to, in0=of, scalar1=-BETA)
 
         def regroup_w2(g, first, tiles):
-            to = w2_grouped[g][:].rearrange("p (t q j) -> p t q j", t=PACK, j=PACK)
-            of = w2_rows[g][:].rearrange("p j (q t) -> p t q j", t=PACK)
-            to, of = to[:, first : first + tiles, :, :], of[:, first : first + tiles, :, :]
-            nc.vector.tensor_copy(out=to[:, :, :VECTOR_Q, :], in_=of[:, :, :VECTOR_Q, :])
-            nc.scalar.copy(out=to[:, :, VECTOR_Q:, :], in_=of[:, :, VECTOR_Q:, :])
+            to = w2_grouped[g][:].rearrange("p (t q i j) -> p t q j i", t=PACK, i=2, j=PACK)
+            of = w2_rows[g][:].rearrange("p j (q i t) -> p t q j i", i=2, t=PACK)
+            for t in range(first, first + tiles):
+                for copy, pairs in (
+                    (nc.vector.tensor_copy, slice(0, VECTOR_Q // 2)),
+                    (nc.scalar.copy, slice(VECTOR_Q // 2, P // 2)),
+                ):
+                    copy(out=to[:, t, pairs, :, :], in_=of[:, t, pairs, :, :])
 
         def quantise(codes, scales, grouped):
             nc.vector.quantize_mx(out=codes.bitcast(FP8X4), scales=scales, in_=grouped)

@@ -142,14 +142,14 @@ def tile_ace_pa_s_kernel(tc, h_enc, enc_w2, enc_b2, clus_w, clus_b, z_out, conf_
             nc.vector.tensor_scalar_mul(out=to, in0=of, scalar1=-BETA)
 
         def regroup_w2(g, first, tiles):
-            to = w2_grouped[g][:].rearrange("p (t q i j) -> p t q j i", t=PACK, i=2, j=PACK)
-            of = w2_rows[g][:].rearrange("p j (q i t) -> p t q j i", i=2, t=PACK)
-            for t in range(first, first + tiles):
-                for copy, pairs in (
-                    (nc.vector.tensor_copy, slice(0, VECTOR_Q // 2)),
-                    (nc.scalar.copy, slice(VECTOR_Q // 2, P // 2)),
-                ):
-                    copy(out=to[:, t, pairs, :, :], in_=of[:, t, pairs, :, :])
+            to = w2_grouped[g][:].rearrange("p (t q i j) -> p q j i t", t=PACK, i=2, j=PACK)
+            of = w2_rows[g][:].rearrange("p j (q i t) -> p q j i t", i=2, t=PACK)
+            tiles = slice(first, first + tiles)
+            for copy, pairs in (
+                (nc.vector.tensor_copy, slice(0, VECTOR_Q // 2)),
+                (nc.scalar.copy, slice(VECTOR_Q // 2, P // 2)),
+            ):
+                copy(out=to[:, pairs, :, :, tiles], in_=of[:, pairs, :, :, tiles])
 
         def quantise(codes, scales, grouped):
             nc.vector.quantize_mx(out=codes.bitcast(FP8X4), scales=scales, in_=grouped)

@@ -203,6 +203,14 @@ def tile_ace_pa_s_kernel(tc, h_enc, enc_w2, enc_b2, clus_w, clus_b, z_out, conf_
         def quantise_chunk(j):
             quantise(cw_codes[j][:], cw_scales[j][:], cw_grouped[j][:])
 
+        def quantise_half(j, half):
+            columns = slice(half * CHUNK_ROWS // 2, (half + 1) * CHUNK_ROWS // 2)
+            quantise(
+                cw_codes[j][:, columns],
+                cw_scales[j][:, columns],
+                cw_grouped[j][:, half * CHUNK_ROWS * PACK // 2 : (half + 1) * CHUNK_ROWS * PACK // 2],
+            )
+
         def multiply_chunk(j):
             sums = psum_mx.tile([P, CHUNK_ROWS], F32, name="sums", tag="mx")
             nc.tensor.matmul_mx(
@@ -216,39 +224,44 @@ def tile_ace_pa_s_kernel(tc, h_enc, enc_w2, enc_b2, clus_w, clus_b, z_out, conf_
             )
             return sums
 
-        def groups_of(j):
-            modules = CHUNK_MODULES if j < CHUNKS - 2 else GROUP_MODULES
-            return [(first, modules) for first in range(0, CHUNK_MODULES, modules)]
+        def scale_modules(j, sums, first, modules):
+            p = 32 * j + 4 * first
+            nc.vector.scalar_tensor_tensor(
+                out=by_slot(scaled[j][:], first, modules),
+                in0=by_slot(sums[:], first, modules),
+                scalar=-BETA,
+                in1=bias_rows[:, :, p : p + 4 * modules],
+                op0=ALU.mult,
+                op1=ALU.add,
+            )
 
-        def scale_chunk(j, sums):
-            for first, modules in groups_of(j):
-                p = 32 * j + 4 * first
-                nc.vector.scalar_tensor_tensor(
-                    out=by_slot(scaled[j][:], first, modules),
-                    in0=by_slot(sums[:], first, modules),
-                    scalar=-BETA,
-                    in1=bias_rows[:, :, p : p + 4 * modules],
-                    op0=ALU.mult,
-                    op1=ALU.add,
-                )
+        def scale_chunk_beside_vector(j, sums):
+            unbiased = keep.tile([P, CHUNK_ROWS], F32)
+            nc.scalar.activation(out=unbiased[:], in_=sums[:], func=ACT.Copy, scale=-BETA)
+            nc.gpsimd.tensor_tensor(
+                out=by_slot(scaled[j][:], 0, CHUNK_MODULES),
+                in0=by_slot(unbiased[:], 0, CHUNK_MODULES),
+                in1=bias_rows[:, :, 32 * j : 32 * (j + 1)],
+                op=ALU.add,
+            )
 
-        def max_chunk(j):
-            for first, modules in groups_of(j):
-                c = j * CHUNK_MODULES + first
-                nc.vector.tensor_reduce(
-                    out=neg_max[:, c : c + modules],
-                    in_=by_module(scaled[j][:])[:, first : first + modules, :, :],
-                    axis=AXIS.XY,
-                    op=ALU.max,
-                    negate=True,
-                )
+        def max_modules(j, first, modules):
+            c = j * CHUNK_MODULES + first
+            nc.vector.tensor_reduce(
+                out=neg_max[:, c : c + modules],
+                in_=by_module(scaled[j][:])[:, first : first + modules, :, :],
+                axis=AXIS.XY,
+                op=ALU.max,
+                negate=True,
+            )
 
-        def sum_exps_chunk(j):
-            exps = keep.tile([P, CHUNK_ROWS], F32, name="exps%d" % j)
-            for m in range(CHUNK_MODULES):
+        exps = [keep.tile([P, CHUNK_ROWS], F32, name="exps%d" % j) for j in range(CHUNKS)]
+
+        def sum_exps_modules(j, first, modules):
+            for m in range(first, first + modules):
                 c = j * CHUNK_MODULES + m
                 nc.scalar.activation(
-                    out=by_module(exps[:])[:, m, :, :],
+                    out=by_module(exps[j][:])[:, m, :, :],
                     in_=by_module(scaled[j][:])[:, m, :, :],
                     func=ACT.Exp,
                     bias=neg_max[:, c : c + 1],
@@ -297,6 +310,7 @@ def tile_ace_pa_s_kernel(tc, h_enc, enc_w2, enc_b2, clus_w, clus_b, z_out, conf_
                     stop=(g == HIDDEN_PASSES - 1),
                 )
         regroup_chunk(0, halves0)
+        quantise_half(0, 0)
         nc.vector.tensor_tensor(
             out=z_grouped[:].rearrange("q (b t) -> q b t", t=PACK),
             in0=zT_sums[:].rearrange("q t b -> q b t"),
@@ -304,31 +318,36 @@ def tile_ace_pa_s_kernel(tc, h_enc, enc_w2, enc_b2, clus_w, clus_b, z_out, conf_
             op=ALU.add,
         )
         halves1 = transpose_chunk(1)
-        quantise_chunk(0)
+        quantise_half(0, 1)
         quantise(z_codes[:], z_scales[:], z_grouped[:])
         regroup_chunk(1, halves1)
         halves2 = transpose_chunk(2)
-        quantise_chunk(1)
+        quantise_half(1, 0)
+        quantise_half(1, 1)
 
+        G = GROUP_MODULES
         sums0 = multiply_chunk(0)
         regroup_chunk(2, halves2)
         halves3 = transpose_chunk(3)
-        scale_chunk(0, sums0)
+        scale_modules(0, sums0, 0, CHUNK_MODULES)
         sums1 = multiply_chunk(1)
         quantise_chunk(2)
-        max_chunk(0)
+        max_modules(0, 0, CHUNK_MODULES)
         regroup_chunk(3, halves3)
-        sum_exps_chunk(0)
-        scale_chunk(1, sums1)
+        scale_chunk_beside_vector(1, sums1)
+        sum_exps_modules(0, 0, CHUNK_MODULES)
         sums2 = multiply_chunk(2)
         quantise_chunk(3)
-        max_chunk(1)
-        sum_exps_chunk(1)
-        scale_chunk(2, sums2)
+        scale_modules(2, sums2, 0, G)
+        scale_modules(2, sums2, G, G)
         sums3 = multiply_chunk(3)
-        max_chunk(2)
-        sum_exps_chunk(2)
-        scale_chunk(3, sums3)
+        max_modules(2, 0, G)
+        max_modules(2, G, G)
+        sum_exps_modules(2, 0, CHUNK_MODULES)
+        scale_modules(3, sums3, 0, G)
+        max_modules(1, 0, CHUNK_MODULES)
+        sum_exps_modules(1, 0, CHUNK_MODULES)
+        scale_modules(3, sums3, G, G)
         z_sums = psum_mx.tile([P, LATENT_TILES, P], F32, name="z_sums", tag="mx")
         for g in range(HIDDEN_PASSES):
             nc.tensor.matmul_mx(
@@ -340,8 +359,9 @@ def tile_ace_pa_s_kernel(tc, h_enc, enc_w2, enc_b2, clus_w, clus_b, z_out, conf_
                 start=(g == 0),
                 stop=(g == HIDDEN_PASSES - 1),
             )
-        max_chunk(3)
-        sum_exps_chunk(3)
+        max_modules(3, 0, G)
+        max_modules(3, G, G)
+        sum_exps_modules(3, 0, CHUNK_MODULES)
 
         z_rows = keep.tile([P, LATENT], F32)
         nc.vector.tensor_tensor(

@@ -235,13 +235,20 @@ def tile_ace_pa_s_kernel(tc, h_enc, enc_w2, enc_b2, clus_w, clus_b, z_out, conf_
                 op1=ALU.add,
             )
 
-        def scale_chunk_beside_vector(j, sums):
-            unbiased = keep.tile([P, CHUNK_ROWS], F32)
-            nc.scalar.activation(out=unbiased[:], in_=sums[:], func=ACT.Copy, scale=-BETA)
+        unbiased = keep.tile([P, CHUNK_ROWS], F32)
+
+        def scale_modules_beside_vector(j, sums, first, modules):
+            p = 32 * j + 4 * first
+            nc.scalar.activation(
+                out=by_slot(unbiased[:], first, modules),
+                in_=by_slot(sums[:], first, modules),
+                func=ACT.Copy,
+                scale=-BETA,
+            )
             nc.gpsimd.tensor_tensor(
-                out=by_slot(scaled[j][:], 0, CHUNK_MODULES),
-                in0=by_slot(unbiased[:], 0, CHUNK_MODULES),
-                in1=bias_rows[:, :, 32 * j : 32 * (j + 1)],
+                out=by_slot(scaled[j][:], first, modules),
+                in0=by_slot(unbiased[:], first, modules),
+                in1=bias_rows[:, :, p : p + 4 * modules],
                 op=ALU.add,
             )
 
@@ -329,24 +336,31 @@ def tile_ace_pa_s_kernel(tc, h_enc, enc_w2, enc_b2, clus_w, clus_b, z_out, conf_
         sums0 = multiply_chunk(0)
         regroup_chunk(2, halves2)
         halves3 = transpose_chunk(3)
-        scale_modules(0, sums0, 0, CHUNK_MODULES)
+        scale_modules(0, sums0, 0, G)
+        scale_modules(0, sums0, G, G)
         sums1 = multiply_chunk(1)
         quantise_chunk(2)
-        max_modules(0, 0, CHUNK_MODULES)
+        max_modules(0, 0, G)
+        max_modules(0, G, G)
         regroup_chunk(3, halves3)
-        scale_chunk_beside_vector(1, sums1)
+        scale_modules_beside_vector(1, sums1, 0, G)
+        scale_modules_beside_vector(1, sums1, G, G)
         sum_exps_modules(0, 0, CHUNK_MODULES)
         sums2 = multiply_chunk(2)
-        quantise_chunk(3)
+        quantise_half(3, 0)
         scale_modules(2, sums2, 0, G)
-        scale_modules(2, sums2, G, G)
+        quantise_half(3, 1)
         sums3 = multiply_chunk(3)
         max_modules(2, 0, G)
+        sum_exps_modules(2, 0, G)
+        scale_modules(2, sums2, G, G)
+        max_modules(1, 0, G)
+        sum_exps_modules(1, 0, G)
         max_modules(2, G, G)
-        sum_exps_modules(2, 0, CHUNK_MODULES)
+        sum_exps_modules(2, G, G)
         scale_modules(3, sums3, 0, G)
-        max_modules(1, 0, CHUNK_MODULES)
-        sum_exps_modules(1, 0, CHUNK_MODULES)
+        max_modules(1, G, G)
+        sum_exps_modules(1, G, G)
         scale_modules(3, sums3, G, G)
         z_sums = psum_mx.tile([P, LATENT_TILES, P], F32, name="z_sums", tag="mx")
         for g in range(HIDDEN_PASSES):

@@ -74,18 +74,16 @@ def tile_ace_pa_s_kernel(tc, h_enc, enc_w2, enc_b2, clus_w, clus_b, z_out, conf_
 
         identity = keep.tile([P, P], F32)
         make_identity(nc, identity[:])
-        zeros = keep.tile([P, P], F32)
-        nc.vector.memset(zeros[:], 0.0)
+        one_column = keep.tile([P, 1], F32)
+        nc.vector.memset(one_column[:], 0.0)
         table_warmer = keep.tile([P, 1], F32)
-        nc.scalar.activation(out=table_warmer[:], in_=zeros[:, :1], func=ACT.Exp)
+        nc.scalar.activation(out=table_warmer[:], in_=one_column[:], func=ACT.Exp)
         unread = psum_mx.tile([P, LATENT], F32, name="unread", tag="mx")
-        nc.tensor.matmul(
-            unread[:].rearrange("p (n c) -> p n c", c=P),
-            lhsT=zeros[:],
-            rhs=zeros[:].unsqueeze(1).to_broadcast([P, LATENT_TILES, P]),
-            start=True,
-            stop=True,
-        )
+
+        def keep_busy(products):
+            for product in range(products):
+                nc.tensor.matmul(unread[:, :P], lhsT=identity[:], rhs=identity[:], start=True, stop=True)
+
         identity_bf16 = keep.tile([P, P], BF16)
         nc.vector.tensor_copy(out=identity_bf16[:], in_=identity[:])
         permutation = keep.tile([P, P], F32)
@@ -275,12 +273,15 @@ def tile_ace_pa_s_kernel(tc, h_enc, enc_w2, enc_b2, clus_w, clus_b, z_out, conf_
                     accum_out=exp_sum[:, c : c + 1],
                 )
 
+        keep_busy(3)
         spread0 = spread_bias(0)
-        spread1 = spread_bias(SLOTS // 2)
+        keep_busy(2)
         regroup_w2(0, 0, LATENT_TILES)
         scale_bias_scalar(bias_rows[:, : SLOTS // 2, :], spread0[:])
         quantise_w2(0, 0, LATENT_TILES)
         h_wordsT = transpose_h()
+        keep_busy(2)
+        spread1 = spread_bias(SLOTS // 2)
         nc.scalar.copy(
             out=h_grouped[:].bitcast(F32).rearrange("q (g b u) -> q g b u", g=HIDDEN_PASSES, u=2),
             in_=h_wordsT[:].rearrange("q g u b -> q g b u"),
@@ -347,20 +348,17 @@ def tile_ace_pa_s_kernel(tc, h_enc, enc_w2, enc_b2, clus_w, clus_b, z_out, conf_
         scale_modules_beside_vector(1, sums1, G, G)
         sum_exps_modules(0, 0, CHUNK_MODULES)
         sums2 = multiply_chunk(2)
-        quantise_half(3, 0)
-        scale_modules(2, sums2, 0, G)
-        quantise_half(3, 1)
+        quantise_chunk(3)
         sums3 = multiply_chunk(3)
-        max_modules(2, 0, G)
-        sum_exps_modules(2, 0, G)
+        scale_modules(2, sums2, 0, G)
         scale_modules(2, sums2, G, G)
-        max_modules(1, 0, G)
-        sum_exps_modules(1, 0, G)
+        max_modules(2, 0, G)
         max_modules(2, G, G)
-        sum_exps_modules(2, G, G)
+        sum_exps_modules(2, 0, CHUNK_MODULES)
         scale_modules(3, sums3, 0, G)
+        max_modules(1, 0, G)
         max_modules(1, G, G)
-        sum_exps_modules(1, G, G)
+        sum_exps_modules(1, 0, CHUNK_MODULES)
         scale_modules(3, sums3, G, G)
         z_sums = psum_mx.tile([P, LATENT_TILES, P], F32, name="z_sums", tag="mx")
         for g in range(HIDDEN_PASSES):

@@ -74,15 +74,15 @@ def tile_ace_pa_s_kernel(tc, h_enc, enc_w2, enc_b2, clus_w, clus_b, z_out, conf_
 
         identity = keep.tile([P, P], F32)
         make_identity(nc, identity[:])
-        one_column = keep.tile([P, 1], F32)
-        nc.vector.memset(one_column[:], 0.0)
+        ones = keep.tile([P, P], F32)
+        nc.vector.memset(ones[:], 1.0)
         table_warmer = keep.tile([P, 1], F32)
-        nc.scalar.activation(out=table_warmer[:], in_=one_column[:], func=ACT.Exp)
-        unread = psum_mx.tile([P, LATENT], F32, name="unread", tag="mx")
+        nc.scalar.activation(out=table_warmer[:], in_=ones[:, :1], func=ACT.Exp)
+        unread = psum_mx.tile([P, P], F32, name="unread", tag="mx")
 
         def keep_busy(products):
             for product in range(products):
-                nc.tensor.matmul(unread[:, :P], lhsT=identity[:], rhs=identity[:], start=True, stop=True)
+                nc.tensor.matmul(unread[:], lhsT=ones[:], rhs=ones[:], start=True, stop=True)
 
         identity_bf16 = keep.tile([P, P], BF16)
         nc.vector.tensor_copy(out=identity_bf16[:], in_=identity[:])
@@ -291,16 +291,6 @@ def tile_ace_pa_s_kernel(tc, h_enc, enc_w2, enc_b2, clus_w, clus_b, z_out, conf_
         quantise(h_codes[:], h_scales[:], h_grouped[:])
         quantise_w2(1, 0, 2)
         quantise_w2(1, 2, 2)
-        for warm in range(2):
-            nc.tensor.matmul_mx(
-                out=unread[:],
-                lhsT=w2_codes[0][:, :P].bitcast(FP8X4),
-                lhsT_scale=w2_scales[0][:, :P],
-                rhs=w2_codes[0][:].bitcast(FP8X4),
-                rhs_scale=w2_scales[0][:],
-                start=True,
-                stop=True,
-            )
         halves0 = transpose_chunk(0)
         scale_bias_scalar(bias_rows[:, SLOTS // 2 : 3 * SLOTS // 4, :], spread1[:, : SLOTS // 4, :])
         scale_bias_vector(bias_rows[:, 3 * SLOTS // 4 :, :], spread1[:, SLOTS // 4 :, :])
@@ -357,8 +347,7 @@ def tile_ace_pa_s_kernel(tc, h_enc, enc_w2, enc_b2, clus_w, clus_b, z_out, conf_
         sum_exps_modules(2, 0, CHUNK_MODULES)
         scale_modules(3, sums3, 0, G)
         max_modules(1, 0, G)
-        max_modules(1, G, G)
-        sum_exps_modules(1, 0, CHUNK_MODULES)
+        sum_exps_modules(1, 0, G)
         scale_modules(3, sums3, G, G)
         z_sums = psum_mx.tile([P, LATENT_TILES, P], F32, name="z_sums", tag="mx")
         for g in range(HIDDEN_PASSES):
@@ -372,8 +361,11 @@ def tile_ace_pa_s_kernel(tc, h_enc, enc_w2, enc_b2, clus_w, clus_b, z_out, conf_
                 stop=(g == HIDDEN_PASSES - 1),
             )
         max_modules(3, 0, G)
+        sum_exps_modules(3, 0, G)
+        max_modules(1, G, G)
+        sum_exps_modules(1, G, G)
         max_modules(3, G, G)
-        sum_exps_modules(3, 0, CHUNK_MODULES)
+        sum_exps_modules(3, G, G)
 
         z_rows = keep.tile([P, LATENT], F32)
         nc.vector.tensor_tensor(

from contextlib import ExitStack

import concourse.mybir as mybir
from concourse.masks import make_identity

F32 = mybir.dt.float32
BF16 = mybir.dt.bfloat16
U32 = mybir.dt.uint32
U8 = mybir.dt.uint8
FP8X4 = mybir.dt.float8_e4m3fn_x4
ALU = mybir.AluOpType
ACT = mybir.ActivationFunctionType
AXIS = mybir.AxisListType

P = 128
PACK = 4
K_PASS = P * PACK
HIDDEN = 1024
LATENT = 512
MODULES = 32
HEADS = 64
BETA = 10.0

HIDDEN_PASSES = HIDDEN // K_PASS
LATENT_TILES = LATENT // P
CHUNK_ROWS = 512
CHUNKS = MODULES * HEADS // CHUNK_ROWS
ROWS_PER_PARTITION = CHUNK_ROWS // P
CHUNK_MODULES = CHUNK_ROWS // HEADS
SLOTS = 16
GROUP_MODULES = CHUNK_MODULES // 2
VECTOR_Q = 96

FLOPS = 2 * P * HIDDEN * LATENT + 2 * P * LATENT * MODULES * HEADS


def tile_ace_pa_s_kernel(tc, h_enc, enc_w2, enc_b2, clus_w, clus_b, z_out, conf_out):
    nc = tc.nc
    with ExitStack() as stack:
        keep = stack.enter_context(tc.tile_pool(name="keep", bufs=1))
        psum_t = stack.enter_context(tc.psum_pool(name="psum_t", bufs=5))
        psum_mx = stack.enter_context(tc.psum_pool(name="psum_mx", bufs=3))
        stack.enter_context(tc.manual_schedule())

        cb = keep.tile([P, SLOTS], BF16)
        nc.sync.dma_start(
            out=cb[:], in_=clus_b.rearrange("c k -> (c k)").rearrange("(p r) -> p r", r=SLOTS)
        )
        w2_rows = []
        for g in range(HIDDEN_PASSES):
            rows = keep.tile([P, PACK, LATENT], BF16, name="w2_rows%d" % g)
            nc.sync.dma_start(
                out=rows[:],
                in_=enc_w2[g * K_PASS : (g + 1) * K_PASS, :].rearrange("(q t) d -> q t d", t=PACK),
            )
            w2_rows.append(rows)
            if g == 0:
                h_rows = keep.tile([P, HIDDEN], BF16)
                nc.sync.dma_start(out=h_rows[:], in_=h_enc)
        b2 = keep.tile([P, PACK], BF16)
        nc.sync.dma_start(out=b2[:], in_=enc_b2.rearrange("(q t) -> q t", t=PACK))
        clus_w_rows = clus_w.rearrange("c k d -> (c k) d")
        cw_rows = []
        for j in range(CHUNKS):
            halves = clus_w_rows[j * CHUNK_ROWS : (j + 1) * CHUNK_ROWS, :].rearrange(
                "(p h r) d -> h p (r d)", h=2, r=2
            )
            for h in range(2):
                rows = keep.tile([P, 2 * LATENT], BF16, name="cw_rows%d_%d" % (j, h))
                nc.sync.dma_start(out=rows[:], in_=halves[h])
                cw_rows.append(rows)
        b2_rows = keep.tile([P, LATENT], BF16)
        nc.sync.dma_start(out=b2_rows[:], in_=enc_b2.partition_broadcast(P))

        identity = keep.tile([P, P], F32)
        make_identity(nc, identity[:])
        ones = keep.tile([P, P], F32)
        nc.vector.memset(ones[:], 1.0)
        table_warmer = keep.tile([P, 1], F32)
        nc.scalar.activation(out=table_warmer[:], in_=ones[:, :1], func=ACT.Exp)
        unread = psum_mx.tile([P, P], F32, name="unread", tag="mx")

        def keep_busy(products):
            for product in range(products):
                nc.tensor.matmul(unread[:], lhsT=ones[:], rhs=ones[:], start=True, stop=True)

        identity_bf16 = keep.tile([P, P], BF16)
        nc.vector.tensor_copy(out=identity_bf16[:], in_=identity[:])
        permutation = keep.tile([P, P], F32)
        nc.vector.tensor_copy(
            out=permutation[:].rearrange("k (o i) -> k o i", o=4),
            in_=identity[:].rearrange("k (i o) -> k o i", o=4),
        )

        bias_rows = keep.tile([P, SLOTS, P], F32)
        w2_grouped = [
            keep.tile([P, LATENT * PACK], BF16, align_bytes=64, name="w2_grouped%d" % g)
            for g in range(HIDDEN_PASSES)
        ]
        w2_codes = [
            keep.tile([P, LATENT], U32, align_bytes=64, name="w2_codes%d" % g) for g in range(HIDDEN_PASSES)
        ]
        w2_scales = [
            keep.tile([P, LATENT], U8, align_bytes=64, name="w2_scales%d" % g) for g in range(HIDDEN_PASSES)
        ]
        h_grouped = keep.tile([P, HIDDEN_PASSES * P * PACK], BF16, align_bytes=64)
        h_codes = keep.tile([P, HIDDEN_PASSES * P], U32, align_bytes=64)
        h_scales = keep.tile([P, HIDDEN_PASSES * P], U8, align_bytes=64)
        z_grouped = keep.tile([P, P * PACK], BF16, align_bytes=64)
        z_codes = keep.tile([P, P], U32, align_bytes=64)
        z_scales = keep.tile([P, P], U8, align_bytes=64)
        cw_grouped = [
            keep.tile([P, CHUNK_ROWS * PACK], BF16, align_bytes=64, name="cw_grouped%d" % j)
            for j in range(CHUNKS)
        ]
        cw_codes = [
            keep.tile([P, CHUNK_ROWS], U32, align_bytes=64, name="cw_codes%d" % j) for j in range(CHUNKS)
        ]
        cw_scales = [
            keep.tile([P, CHUNK_ROWS], U8, align_bytes=64, name="cw_scales%d" % j) for j in range(CHUNKS)
        ]
        scaled = [keep.tile([P, CHUNK_ROWS], F32, name="scaled%d" % j) for j in range(CHUNKS)]
        neg_max = keep.tile([P, MODULES], F32)
        exp_sum = keep.tile([P, MODULES], F32)

        def spread_bias(first):
            spread = psum_t.tile([P, SLOTS // 2, P], BF16, name="spread", tag="t")
            for s in range(SLOTS // 2):
                r, o = divmod(first + s, 4)
                column = 4 * o + r
                nc.tensor.transpose(
                    spread[:, s, :], cb[:, column : column + 1].to_broadcast([P, P]), identity_bf16[:]
                )
            return spread

        def scale_bias_scalar(to, of):
            nc.scalar.activation(out=to, in_=of, func=ACT.Copy, scale=-BETA)

        def scale_bias_vector(to, of):
            nc.vector.tensor_scalar_mul(out=to, in0=of, scalar1=-BETA)

        def regroup_w2(g, first, tiles):
            to = w2_grouped[g][:].rearrange("p (t q i j) -> p q j i t", t=PACK, i=2, j=PACK)
            of = w2_rows[g][:].rearrange("p j (q i t) -> p q j i t", i=2, t=PACK)
            tiles = slice(first, first + tiles)
            for copy, pairs in (
                (nc.vector.tensor_copy, slice(0, VECTOR_Q // 2)),
                (nc.scalar.copy, slice(VECTOR_Q // 2, P // 2)),
            ):
                copy(out=to[:, pairs, :, :, tiles], in_=of[:, pairs, :, :, tiles])

        def quantise(codes, scales, grouped):
            nc.vector.quantize_mx(out=codes.bitcast(FP8X4), scales=scales, in_=grouped)

        def quantise_w2(g, first, tiles):
            columns = slice(first * P, (first + tiles) * P)
            quantise(
                w2_codes[g][:, columns],
                w2_scales[g][:, columns],
                w2_grouped[g][:, first * P * PACK : (first + tiles) * P * PACK],
            )

        def transpose_h():
            h_words = h_rows[:].bitcast(F32)
            wordsT = psum_t.tile([P, HIDDEN_PASSES, 2, P], F32, name="h_wordsT", tag="t")
            for g in range(HIDDEN_PASSES):
                for u in range(2):
                    every_2nd = slice(2 * g * P + u, 2 * (g + 1) * P, 2)
                    nc.tensor.transpose(wordsT[:, g, u, :], h_words[:, every_2nd], identity[:])
            return wordsT

        def by_module(columns):
            return columns.rearrange("b (s m i) -> b m s i", s=SLOTS, m=CHUNK_MODULES)

        def by_slot(columns, first, modules):
            columns = columns.rearrange("b (s m i) -> b s m i", s=SLOTS, m=CHUNK_MODULES)
            return columns[:, :, first : first + modules, :].rearrange("b s m i -> b s (m i)")

        def transpose_half(j, half):
            words = cw_rows[2 * j + half][:].bitcast(F32)
            wordsT = psum_t.tile([P, 2, 2, P], F32, name="cw_wordsT", tag="t")
            for r in range(2):
                for u in range(2):
                    every_2nd = slice(2 * r * P + u, 2 * (r + 1) * P, 2)
                    nc.tensor.transpose(wordsT[:, r, u, :], words[:, every_2nd], permutation[:])
            return wordsT

        def transpose_chunk(j):
            return [transpose_half(j, half) for half in range(2)]

        def regroup_chunk(j, halves):
            grouped_words = cw_grouped[j][:].bitcast(F32).rearrange(
                "q (r p u) -> q r p u", r=ROWS_PER_PARTITION, u=2
            )
            for half in range(2):
                nc.scalar.copy(
                    out=grouped_words[:, 2 * half : 2 * half + 2, :, :],
                    in_=halves[half][:].rearrange("q r u p -> q r p u"),
                )

        def quantise_chunk(j):
            quantise(cw_codes[j][:], cw_scales[j][:], cw_grouped[j][:])

        def quantise_half(j, half):
            columns = slice(half * CHUNK_ROWS // 2, (half + 1) * CHUNK_ROWS // 2)
            quantise(
                cw_codes[j][:, columns],
                cw_scales[j][:, columns],
                cw_grouped[j][:, half * CHUNK_ROWS * PACK // 2 : (half + 1) * CHUNK_ROWS * PACK // 2],
            )

        def multiply_chunk(j):
            sums = psum_mx.tile([P, CHUNK_ROWS], F32, name="sums", tag="mx")
            nc.tensor.matmul_mx(
                out=sums[:],
                lhsT=z_codes[:].bitcast(FP8X4),
                lhsT_scale=z_scales[:],
                rhs=cw_codes[j][:].bitcast(FP8X4),
                rhs_scale=cw_scales[j][:],
                start=True,
                stop=True,
            )
            return sums

        def scale_modules(j, sums, first, modules):
            p = 32 * j + 4 * first
            nc.vector.scalar_tensor_tensor(
                out=by_slot(scaled[j][:], first, modules),
                in0=by_slot(sums[:], first, modules),
                scalar=-BETA,
                in1=bias_rows[:, :, p : p + 4 * modules],
                op0=ALU.mult,
                op1=ALU.add,
            )

        unbiased = keep.tile([P, CHUNK_ROWS], F32)

        def scale_modules_beside_vector(j, sums, first, modules):
            p = 32 * j + 4 * first
            nc.scalar.activation(
                out=by_slot(unbiased[:], first, modules),
                in_=by_slot(sums[:], first, modules),
                func=ACT.Copy,
                scale=-BETA,
            )
            nc.gpsimd.tensor_tensor(
                out=by_slot(scaled[j][:], first, modules),
                in0=by_slot(unbiased[:], first, modules),
                in1=bias_rows[:, :, p : p + 4 * modules],
                op=ALU.add,
            )

        def max_modules(j, first, modules):
            c = j * CHUNK_MODULES + first
            nc.vector.tensor_reduce(
                out=neg_max[:, c : c + modules],
                in_=by_module(scaled[j][:])[:, first : first + modules, :, :],
                axis=AXIS.XY,
                op=ALU.max,
                negate=True,
            )

        exps = [keep.tile([P, CHUNK_ROWS], F32, name="exps%d" % j) for j in range(CHUNKS)]

        def sum_exps_modules(j, first, modules):
            for m in range(first, first + modules):
                c = j * CHUNK_MODULES + m
                nc.scalar.activation(
                    out=by_module(exps[j][:])[:, m, :, :],
                    in_=by_module(scaled[j][:])[:, m, :, :],
                    func=ACT.Exp,
                    bias=neg_max[:, c : c + 1],
                    accum_out=exp_sum[:, c : c + 1],
                )

        keep_busy(3)
        spread0 = spread_bias(0)
        keep_busy(2)
        regroup_w2(0, 0, LATENT_TILES)
        scale_bias_scalar(bias_rows[:, : SLOTS // 2, :], spread0[:])
        quantise_w2(0, 0, LATENT_TILES)
        h_wordsT = transpose_h()
        keep_busy(2)
        spread1 = spread_bias(SLOTS // 2)
        nc.scalar.copy(
            out=h_grouped[:].bitcast(F32).rearrange("q (g b u) -> q g b u", g=HIDDEN_PASSES, u=2),
            in_=h_wordsT[:].rearrange("q g u b -> q g b u"),
        )
        regroup_w2(1, 0, 2)
        regroup_w2(1, 2, 2)
        quantise(h_codes[:], h_scales[:], h_grouped[:])
        quantise_w2(1, 0, 2)
        quantise_w2(1, 2, 2)
        halves0 = transpose_chunk(0)
        scale_bias_scalar(bias_rows[:, SLOTS // 2 : 3 * SLOTS // 4, :], spread1[:, : SLOTS // 4, :])
        scale_bias_vector(bias_rows[:, 3 * SLOTS // 4 :, :], spread1[:, SLOTS // 4 :, :])

        zT_sums = psum_mx.tile([P, LATENT_TILES, P], F32, name="zT_sums", tag="mx")
        for t in range(LATENT_TILES):
            for g in range(HIDDEN_PASSES):
                nc.tensor.matmul_mx(
                    out=zT_sums[:, t, :],
                    lhsT=w2_codes[g][:, t * P : (t + 1) * P].bitcast(FP8X4),
                    lhsT_scale=w2_scales[g][:, t * P : (t + 1) * P],
                    rhs=h_codes[:, g * P : (g + 1) * P].bitcast(FP8X4),
                    rhs_scale=h_scales[:, g * P : (g + 1) * P],
                    start=(g == 0),
                    stop=(g == HIDDEN_PASSES - 1),
                )
        regroup_chunk(0, halves0)
        quantise_half(0, 0)
        nc.vector.tensor_tensor(
            out=z_grouped[:].rearrange("q (b t) -> q b t", t=PACK),
            in0=zT_sums[:].rearrange("q t b -> q b t"),
            in1=b2[:].unsqueeze(1).to_broadcast([P, P, PACK]),
            op=ALU.add,
        )
        halves1 = transpose_chunk(1)
        quantise_half(0, 1)
        quantise(z_codes[:], z_scales[:], z_grouped[:])
        regroup_chunk(1, halves1)
        halves2 = transpose_chunk(2)
        quantise_half(1, 0)
        quantise_half(1, 1)

        G = GROUP_MODULES
        sums0 = multiply_chunk(0)
        regroup_chunk(2, halves2)
        halves3 = transpose_chunk(3)
        scale_modules(0, sums0, 0, G)
        scale_modules(0, sums0, G, G)
        sums1 = multiply_chunk(1)
        quantise_chunk(2)
        max_modules(0, 0, G)
        max_modules(0, G, G)
        regroup_chunk(3, halves3)
        scale_modules_beside_vector(1, sums1, 0, G)
        scale_modules_beside_vector(1, sums1, G, G)
        sum_exps_modules(0, 0, CHUNK_MODULES)
        sums2 = multiply_chunk(2)
        quantise_chunk(3)
        sums3 = multiply_chunk(3)
        scale_modules(2, sums2, 0, G)
        scale_modules(2, sums2, G, G)
        max_modules(2, 0, G)
        max_modules(2, G, G)
        sum_exps_modules(2, 0, CHUNK_MODULES)
        scale_modules(3, sums3, 0, G)
        max_modules(1, 0, G)
        sum_exps_modules(1, 0, G)
        scale_modules(3, sums3, G, G)
        z_sums = psum_mx.tile([P, LATENT_TILES, P], F32, name="z_sums", tag="mx")
        for g in range(HIDDEN_PASSES):
            nc.tensor.matmul_mx(
                out=z_sums[:].rearrange("b t q -> b (t q)"),
                lhsT=h_codes[:, g * P : (g + 1) * P].bitcast(FP8X4),
                lhsT_scale=h_scales[:, g * P : (g + 1) * P],
                rhs=w2_codes[g][:].bitcast(FP8X4),
                rhs_scale=w2_scales[g][:],
                start=(g == 0),
                stop=(g == HIDDEN_PASSES - 1),
            )
        max_modules(3, 0, G)
        sum_exps_modules(3, 0, G)
        max_modules(1, G, G)
        sum_exps_modules(1, G, G)
        max_modules(3, G, G)
        sum_exps_modules(3, G, G)

        z_rows = keep.tile([P, LATENT], F32)
        nc.vector.tensor_tensor(
            out=z_rows[:].rearrange("b (q t) -> b q t", t=PACK),
            in0=z_sums[:].rearrange("b t q -> b q t"),
            in1=b2_rows[:].rearrange("b (q t) -> b q t", t=PACK),
            op=ALU.add,
        )
        nc.sync.dma_start(out=z_out, in_=z_rows[:])

        log_sum = keep.tile([P, MODULES], F32)
        nc.scalar.activation(out=log_sum[:], in_=exp_sum[:], func=ACT.Ln)
        conf = keep.tile([P, MODULES], F32)
        nc.vector.tensor_sub(out=conf[:], in0=neg_max[:], in1=log_sum[:])
        nc.sync.dma_start(out=conf_out, in_=conf[:])
